import numpy as np
import ml_dtypes


def mxq(x, axis, fmt="e4m3"):
    dtype, down = {"e4m3": (ml_dtypes.float8_e4m3fn, 7), "e5m2": (ml_dtypes.float8_e5m2, 14)}[fmt]
    v = np.moveaxis(np.asarray(x, np.float32).astype(ml_dtypes.bfloat16).astype(np.float64), axis, -1)
    blocks = v.reshape(v.shape[:-1] + (-1, 32))
    amax = np.abs(blocks).max(-1, keepdims=True)
    byte = np.maximum(np.where(amax > 0, np.frexp(amax)[1] - 1 + 127, 0) - down, 1)
    scale = np.exp2(byte - 127.0)
    codes = (blocks / scale).astype(np.float32).astype(dtype).astype(np.float64)
    return np.moveaxis((codes * scale).reshape(v.shape), -1, axis)


WIDE = False


def mx_kscale(k):
    if not WIDE:
        return np.ones(k)
    levels = np.array([10, -10, 5, -5, 0])
    a = np.random.permutation(np.resize(levels, k // 512 * 4)).reshape(k // 512, 4)
    idx = np.arange(k)
    return np.exp2(a[idx // 512, idx % 128 // 32])


BF16 = ml_dtypes.bfloat16


def bf(x):
    return np.asarray(x, np.float32).astype(BF16)


def f64(x):
    return np.asarray(x).astype(np.float64)


N, D, H, Z = 512, 1024, 8, 128
BETA = 1.0 / np.sqrt(Z)


def setup_inputs():
    fs = 2.0 * np.sqrt(Z / D)
    s = mx_kscale(N)
    c = 0.5 * np.sqrt(Z)
    K = np.random.standard_normal((N, H, Z)) * 1.4
    Q = np.random.standard_normal((N, H, Z)) * 1.4
    F1 = np.random.standard_normal((N, H, D)) * fs
    F2 = np.random.standard_normal((N, H, D)) * fs
    Q[:, :, 0] = c
    K[:, :, 0] += (np.log(s) / (BETA * c))[:, None]
    F1 = F1 * (s.max() / s)[:, None, None]
    return {"K": bf(K), "Q": bf(Q), "F1": bf(F1), "F2": bf(F2)}


def reference(K, Q, F1, F2):
    Kh = f64(K).transpose(1, 0, 2)
    Qh = f64(Q).transpose(1, 0, 2)
    A1 = BETA * (Qh @ Kh.transpose(0, 2, 1))
    e = np.exp(A1 - A1.max(-1, keepdims=True))
    A2 = e / e.sum(-1, keepdims=True)
    T1 = -(mxq(A2, 2, "e4m3") @ mxq(f64(F1).transpose(1, 0, 2), 1, "e4m3")).sum(0)
    T2 = -(mxq(A2.transpose(0, 2, 1), 2, "e4m3") @ mxq(f64(F2).transpose(1, 0, 2), 1, "e4m3")).sum(0)
    return T1 + T2

@@ -1,0 +1,279 @@
+from contextlib import ExitStack
+
+import concourse.mybir as mybir
+from concourse.masks import make_identity
+
+BF16 = mybir.dt.bfloat16
+F32 = mybir.dt.float32
+U32 = mybir.dt.uint32
+U8 = mybir.dt.uint8
+FP8X4 = mybir.dt.float8_e4m3fn_x4
+ALU = mybir.AluOpType
+ACT = mybir.ActivationFunctionType
+
+P = 128
+PACK = 4
+TOKENS = P * PACK
+HEADS = 8
+Z = 128
+D = 1024
+HALF = 512
+HALVES = D // HALF
+BETA = 1.0 / (Z**0.5)
+RUN = 4
+HEAD_CUTS = (0, 1, 4, 8)
+AHEAD = 9
+
+FLOPS = 2 * HEADS * TOKENS * TOKENS * Z + 2 * 2 * HEADS * TOKENS * TOKENS * D
+
+
+def words_first(grouped):
+    return grouped.rearrange("p (c i) t -> p c t i", i=RUN)
+
+
+def rows_first(raw):
+    return raw.rearrange("p t (c i) -> p c t i", i=RUN)
+
+
+def tile_multiheadattention_pa_kernel(tc, K, Q, F1, F2, out):
+    nc = tc.nc
+
+    q_rows = Q.rearrange("(p j) h z -> p j h z", j=PACK)
+    k_rows = K.rearrange("(p j) h z -> p j h z", j=PACK)
+    f1_rows = F1.rearrange("(p j) h d -> p j h d", j=PACK)
+    f2_rows = F2.rearrange("(p j) h d -> p j h d", j=PACK)
+    out_rows = out.rearrange("(p j) d -> p j d", j=PACK)
+
+    steps = [(half, h) for half in range(HALVES) for h in range(HEADS)]
+
+    with ExitStack() as ctx:
+        ctx.enter_context(tc.manual_schedule())
+        keep = ctx.enter_context(tc.tile_pool(name="keep", bufs=1))
+        raw_pool = ctx.enter_context(tc.tile_pool(name="raw", bufs=AHEAD + 1))
+        soft = ctx.enter_context(tc.tile_pool(name="soft", bufs=2))
+        stage = ctx.enter_context(tc.tile_pool(name="stage", bufs=3))
+        results = ctx.enter_context(tc.tile_pool(name="results", bufs=PACK))
+        acc_pool = ctx.enter_context(tc.psum_pool(name="acc", bufs=1))
+        work = ctx.enter_context(tc.psum_pool(name="work", bufs=2))
+
+        q_raw = keep.tile([P, PACK, HEADS, Z], BF16)
+        k_raw = keep.tile([P, PACK, HEADS, Z], BF16)
+        for first, last in zip(HEAD_CUTS[:-1], HEAD_CUTS[1:]):
+            nc.sync.dma_start(out=k_raw[:, :, first:last, :], in_=k_rows[:, :, first:last, :])
+            nc.sync.dma_start(out=q_raw[:, :, first:last, :], in_=q_rows[:, :, first:last, :])
+
+        ident = keep.tile([P, P], BF16)
+        make_identity(nc, ident[:])
+
+        by_key_codes = keep.tile([P, HEADS, TOKENS], U32, align_bytes=64)
+        by_key_scales = keep.tile([P, HEADS, TOKENS], U8, align_bytes=64)
+        by_query_codes = keep.tile([P, HEADS, TOKENS], U32, align_bytes=64)
+        by_query_scales = keep.tile([P, HEADS, TOKENS], U8, align_bytes=64)
+
+        f_raw = {}
+        f_grouped = {}
+        f_quantised = {}
+        flipped_qk = {}
+        qk_t = {}
+        scores = {}
+        expo = {}
+        shift = {}
+        sums = {}
+
+        def quantise(grouped, codes, scales):
+            nc.vector.quantize_mx(out=codes.bitcast(FP8X4), scales=scales, in_=grouped)
+
+        def load_step(s):
+            half, h = steps[s]
+            cols = slice(half * HALF, (half + 1) * HALF)
+            f1_raw = raw_pool.tile([P, PACK, HALF], BF16)
+            nc.sync.dma_start(out=f1_raw[:], in_=f1_rows[:, :, h, cols])
+            f2_raw = raw_pool.tile([P, PACK, HALF], BF16)
+            nc.sync.dma_start(out=f2_raw[:], in_=f2_rows[:, :, h, cols])
+            f_raw[s] = (f1_raw, f2_raw)
+
+        def regroup_step(s):
+            f1_raw, f2_raw = f_raw.pop(s)
+            f1_grouped = stage.tile([P, HALF, PACK], BF16, align_bytes=64)
+            nc.vector.tensor_copy(out=words_first(f1_grouped[:]), in_=rows_first(f1_raw[:]))
+            f2_grouped = stage.tile([P, HALF, PACK], BF16, align_bytes=64)
+            nc.scalar.copy(out=words_first(f2_grouped[:]), in_=rows_first(f2_raw[:]))
+            f_grouped[s] = (f1_grouped, f2_grouped)
+
+        def quantise_step(s):
+            f1_grouped, f2_grouped = f_grouped.pop(s)
+            f1_codes = stage.tile([P, HALF], U32, align_bytes=64)
+            f1_scales = stage.tile([P, HALF], U8, align_bytes=64)
+            quantise(f1_grouped[:].rearrange("p c t -> p (c t)"), f1_codes[:], f1_scales[:])
+            f2_codes = stage.tile([P, HALF], U32, align_bytes=64)
+            f2_scales = stage.tile([P, HALF], U8, align_bytes=64)
+            quantise(f2_grouped[:].rearrange("p c t -> p (c t)"), f2_codes[:], f2_scales[:])
+            f_quantised[s] = (f1_codes, f1_scales, f2_codes, f2_scales)
+
+        def multiply_step(s, acc):
+            half, h = steps[s]
+            f1_codes, f1_scales, f2_codes, f2_scales = f_quantised.pop(s)
+            for i in range(PACK):
+                rows = slice(i * P, (i + 1) * P)
+                nc.tensor.matmul_mx(
+                    out=acc[i][:],
+                    lhsT=by_key_codes[:, h, rows].bitcast(FP8X4),
+                    lhsT_scale=by_key_scales[:, h, rows],
+                    rhs=f1_codes[:].bitcast(FP8X4),
+                    rhs_scale=f1_scales[:],
+                    start=(h == 0),
+                    stop=False,
+                )
+            for i in range(PACK):
+                rows = slice(i * P, (i + 1) * P)
+                nc.tensor.matmul_mx(
+                    out=acc[i][:],
+                    lhsT=by_query_codes[:, h, rows].bitcast(FP8X4),
+                    lhsT_scale=by_query_scales[:, h, rows],
+                    rhs=f2_codes[:].bitcast(FP8X4),
+                    rhs_scale=f2_scales[:],
+                    start=False,
+                    stop=(h == HEADS - 1),
+                )
+
+        def store_half(half, acc):
+            cols = slice(half * HALF, (half + 1) * HALF)
+            for i in range(PACK):
+                result = results.tile([P, HALF], F32)
+                if i % 2 == 0:
+                    nc.scalar.mul(out=result[:], in_=acc[i][:], mul=-1.0)
+                else:
+                    nc.vector.tensor_scalar_mul(out=result[:], in0=acc[i][:], scalar1=-1.0)
+                nc.sync.dma_start(out=out_rows[:, i, cols], in_=result[:])
+
+        def flip_qk(h):
+            flipped = work.tile([P, 2, PACK, P], BF16, tag="flip")
+            for j in range(PACK):
+                nc.tensor.transpose(flipped[:, 0, j, :], q_raw[:, j, h, :], ident[:])
+                nc.tensor.transpose(flipped[:, 1, j, :], k_raw[:, j, h, :], ident[:])
+            flipped_qk[h] = flipped
+
+        def copy_qk(h):
+            qk = soft.tile([P, 2, PACK, P], BF16)
+            nc.scalar.copy(out=qk[:], in_=flipped_qk.pop(h)[:])
+            qk_t[h] = qk
+
+        def score(h, j):
+            bank = work.tile([P, TOKENS], F32, tag="score")
+            nc.tensor.matmul(
+                out=bank[:],
+                lhsT=qk_t[h][:, 0, j, :],
+                rhs=qk_t[h][:, 1, :, :].rearrange("z j m -> z (j m)"),
+                start=True,
+                stop=True,
+            )
+            scores[(h, j)] = bank
+
+        def exponential(h, j):
+            if j == 0:
+                expo[h] = soft.tile([P, PACK, TOKENS], F32, name="expo")
+                shift[h] = soft.tile([P, PACK], F32, name="shift")
+                sums[h] = soft.tile([P, PACK], F32, name="sums")
+            nc.vector.tensor_scalar(
+                out=expo[h][:, j, :],
+                in0=scores.pop((h, j))[:],
+                scalar1=-BETA,
+                scalar2=None,
+                op0=ALU.mult,
+                op1=ALU.min,
+                accum_out=shift[h][:, j : j + 1],
+            )
+            nc.scalar.activation(
+                out=expo[h][:, j, :],
+                in_=expo[h][:, j, :],
+                func=ACT.Exp,
+                bias=shift[h][:, j : j + 1],
+                scale=-1.0,
+                accum_out=sums[h][:, j : j + 1],
+            )
+
+        def normalise_and_flip(h):
+            inverse = soft.tile([P, PACK], F32)
+            nc.vector.reciprocal(out=inverse[:], in_=sums.pop(h)[:])
+            a2 = soft.tile([P, PACK, TOKENS], BF16)
+            for j in range(PACK):
+                nc.vector.tensor_scalar(
+                    out=a2[:, j, :],
+                    in0=expo[h][:, j, :],
+                    scalar1=inverse[:, j : j + 1],
+                    scalar2=None,
+                    op0=ALU.mult,
+                )
+            expo.pop(h)
+            shift.pop(h)
+            by_key = soft.tile([P, PACK, P, PACK], BF16, align_bytes=64)
+            for pair in range(0, PACK, 2):
+                flipped = work.tile([P, 2, PACK, P], BF16, tag="flip")
+                for a in range(2):
+                    for jj in range(PACK):
+                        nc.tensor.transpose(
+                            flipped[:, a, jj, :], a2[:, pair + a, jj * P : (jj + 1) * P], ident[:]
+                        )
+                nc.scalar.copy(
+                    out=by_key[:, pair : pair + 2, :, :],
+                    in_=flipped[:].rearrange("p a t m -> p a m t"),
+                )
+            by_query = soft.tile([P, TOKENS, PACK], BF16, align_bytes=64)
+            nc.vector.tensor_copy(out=words_first(by_query[:]), in_=rows_first(a2[:]))
+            return by_key, by_query
+
+        def quantise_a2(h, by_key, by_query):
+            quantise(
+                by_query[:].rearrange("p c t -> p (c t)"),
+                by_query_codes[:, h, :],
+                by_query_scales[:, h, :],
+            )
+            quantise(
+                by_key[:].rearrange("p j m t -> p (j m t)"),
+                by_key_codes[:, h, :],
+                by_key_scales[:, h, :],
+            )
+
+        for s in range(AHEAD):
+            load_step(s)
+        flip_qk(0)
+        copy_qk(0)
+        score(0, 0)
+        score(0, 1)
+
+        acc_lo = [acc_pool.tile([P, HALF], F32, name="acc_lo%d" % i) for i in range(PACK)]
+        acc_hi = []
+
+        for t in range(len(steps) + 2):
+            if t + AHEAD < len(steps):
+                load_step(t + AHEAD)
+            if t + 1 < HEADS:
+                flip_qk(t + 1)
+            if t < HEADS:
+                exponential(t, 0)
+                score(t, 2)
+                exponential(t, 1)
+                score(t, 3)
+                exponential(t, 2)
+                exponential(t, 3)
+            if t + 1 < HEADS:
+                copy_qk(t + 1)
+            if 1 <= t <= HEADS:
+                by_key, by_query = normalise_and_flip(t - 1)
+            if t == HEADS + 2:
+                acc_hi.extend(work.tile([P, HALF], F32, tag="score", name="acc_hi%d" % i) for i in range(2))
+                acc_hi.extend(work.tile([P, HALF], F32, tag="flip", name="acc_hi%d" % i) for i in range(2, 4))
+            if 2 <= t:
+                multiply_step(t - 2, acc_lo if t - 2 < HEADS else acc_hi)
+            if t + 1 < HEADS:
+                score(t + 1, 0)
+                score(t + 1, 1)
+            if 1 <= t <= len(steps):
+                quantise_step(t - 1)
+            if t < len(steps):
+                regroup_step(t)
+            if 1 <= t <= HEADS:
+                quantise_a2(t - 1, by_key, by_query)
+            if t - 2 == HEADS - 1:
+                store_half(0, acc_lo)
+        store_half(1, acc_hi)

@@ -39,7 +39,7 @@ def tile_multiheadattention_pa_kernel(tc, K, Q, F1, F2, out):
     nc = tc.nc
 
     q_rows = Q.rearrange("(p j) h z -> p j h z", j=PACK)
-    k_rows = K.rearrange("(p j) h z -> p j h z", j=PACK)
+    k_rows = K.rearrange("(j p) h z -> p j h z", p=P)
     f1_rows = F1.rearrange("(p j) h d -> p j h d", j=PACK)
     f2_rows = F2.rearrange("(p j) h d -> p j h d", j=PACK)
     out_rows = out.rearrange("(p j) d -> p j d", j=PACK)
@@ -64,6 +64,8 @@ def tile_multiheadattention_pa_kernel(tc, K, Q, F1, F2, out):
 
         ident = keep.tile([P, P], BF16)
         make_identity(nc, ident[:])
+        ident_words = keep.tile([P, P], F32)
+        make_identity(nc, ident_words[:])
 
         by_key_codes = keep.tile([P, HEADS, TOKENS], U32, align_bytes=64)
         by_key_scales = keep.tile([P, HEADS, TOKENS], U8, align_bytes=64)
@@ -79,6 +81,7 @@ def tile_multiheadattention_pa_kernel(tc, K, Q, F1, F2, out):
         expo = {}
         shift = {}
         sums = {}
+        by_key_of = {}
 
         def quantise(grouped, codes, scales):
             nc.vector.quantize_mx(out=codes.bitcast(FP8X4), scales=scales, in_=grouped)
@@ -92,27 +95,26 @@ def tile_multiheadattention_pa_kernel(tc, K, Q, F1, F2, out):
             nc.sync.dma_start(out=f2_raw[:], in_=f2_rows[:, :, h, cols])
             f_raw[s] = (f1_raw, f2_raw)
 
-        def regroup_step(s):
-            f1_raw, f2_raw = f_raw.pop(s)
-            f1_grouped = stage.tile([P, HALF, PACK], BF16, align_bytes=64)
-            nc.vector.tensor_copy(out=words_first(f1_grouped[:]), in_=rows_first(f1_raw[:]))
+        def regroup_f2(s):
             f2_grouped = stage.tile([P, HALF, PACK], BF16, align_bytes=64)
-            nc.scalar.copy(out=words_first(f2_grouped[:]), in_=rows_first(f2_raw[:]))
-            f_grouped[s] = (f1_grouped, f2_grouped)
+            nc.scalar.copy(out=words_first(f2_grouped[:]), in_=rows_first(f_raw[s][1][:]))
+            f_grouped[(s, 2)] = f2_grouped
 
-        def quantise_step(s):
-            f1_grouped, f2_grouped = f_grouped.pop(s)
-            f1_codes = stage.tile([P, HALF], U32, align_bytes=64)
-            f1_scales = stage.tile([P, HALF], U8, align_bytes=64)
-            quantise(f1_grouped[:].rearrange("p c t -> p (c t)"), f1_codes[:], f1_scales[:])
-            f2_codes = stage.tile([P, HALF], U32, align_bytes=64)
-            f2_scales = stage.tile([P, HALF], U8, align_bytes=64)
-            quantise(f2_grouped[:].rearrange("p c t -> p (c t)"), f2_codes[:], f2_scales[:])
-            f_quantised[s] = (f1_codes, f1_scales, f2_codes, f2_scales)
+        def regroup_f1(s):
+            f1_grouped = stage.tile([P, HALF, PACK], BF16, align_bytes=64)
+            nc.vector.tensor_copy(out=words_first(f1_grouped[:]), in_=rows_first(f_raw.pop(s)[0][:]))
+            f_grouped[(s, 1)] = f1_grouped
+
+        def quantise_f(s, which):
+            codes = stage.tile([P, HALF], U32, align_bytes=64, name="f%d_codes" % which)
+            scales = stage.tile([P, HALF], U8, align_bytes=64, name="f%d_scales" % which)
+            quantise(f_grouped.pop((s, which))[:].rearrange("p c t -> p (c t)"), codes[:], scales[:])
+            f_quantised[(s, which)] = (codes, scales)
 
         def multiply_step(s, acc):
-            half, h = steps[s]
-            f1_codes, f1_scales, f2_codes, f2_scales = f_quantised.pop(s)
+            h = steps[s][1]
+            f1_codes, f1_scales = f_quantised.pop((s, 1))
+            f2_codes, f2_scales = f_quantised.pop((s, 2))
             for i in range(PACK):
                 rows = slice(i * P, (i + 1) * P)
                 nc.tensor.matmul_mx(
@@ -124,8 +126,6 @@ def tile_multiheadattention_pa_kernel(tc, K, Q, F1, F2, out):
                     start=(h == 0),
                     stop=False,
                 )
-            for i in range(PACK):
-                rows = slice(i * P, (i + 1) * P)
                 nc.tensor.matmul_mx(
                     out=acc[i][:],
                     lhsT=by_query_codes[:, h, rows].bitcast(FP8X4),
@@ -169,7 +169,7 @@ def tile_multiheadattention_pa_kernel(tc, K, Q, F1, F2, out):
             )
             scores[(h, j)] = bank
 
-        def exponential(h, j):
+        def shifted(h, j):
             if j == 0:
                 expo[h] = soft.tile([P, PACK, TOKENS], F32, name="expo")
                 shift[h] = soft.tile([P, PACK], F32, name="shift")
@@ -183,6 +183,8 @@ def tile_multiheadattention_pa_kernel(tc, K, Q, F1, F2, out):
                 op1=ALU.min,
                 accum_out=shift[h][:, j : j + 1],
             )
+
+        def exponential(h, j):
             nc.scalar.activation(
                 out=expo[h][:, j, :],
                 in_=expo[h][:, j, :],
@@ -192,11 +194,14 @@ def tile_multiheadattention_pa_kernel(tc, K, Q, F1, F2, out):
                 accum_out=sums[h][:, j : j + 1],
             )
 
-        def normalise_and_flip(h):
+        def invert_sums(h):
             inverse = soft.tile([P, PACK], F32)
             nc.vector.reciprocal(out=inverse[:], in_=sums.pop(h)[:])
             a2 = soft.tile([P, PACK, TOKENS], BF16)
-            for j in range(PACK):
+            return inverse, a2
+
+        def normalise(h, j, inverse, a2):
+            if j < PACK // 2:
                 nc.vector.tensor_scalar(
                     out=a2[:, j, :],
                     in0=expo[h][:, j, :],
@@ -204,32 +209,43 @@ def tile_multiheadattention_pa_kernel(tc, K, Q, F1, F2, out):
                     scalar2=None,
                     op0=ALU.mult,
                 )
-            expo.pop(h)
-            shift.pop(h)
-            by_key = soft.tile([P, PACK, P, PACK], BF16, align_bytes=64)
-            for pair in range(0, PACK, 2):
-                flipped = work.tile([P, 2, PACK, P], BF16, tag="flip")
-                for a in range(2):
-                    for jj in range(PACK):
-                        nc.tensor.transpose(
-                            flipped[:, a, jj, :], a2[:, pair + a, jj * P : (jj + 1) * P], ident[:]
-                        )
-                nc.scalar.copy(
-                    out=by_key[:, pair : pair + 2, :, :],
-                    in_=flipped[:].rearrange("p a t m -> p a m t"),
+            else:
+                nc.scalar.activation(
+                    out=a2[:, j, :], in_=expo[h][:, j, :], func=ACT.Copy, scale=inverse[:, j : j + 1]
                 )
-            by_query = soft.tile([P, TOKENS, PACK], BF16, align_bytes=64)
-            nc.vector.tensor_copy(out=words_first(by_query[:]), in_=rows_first(a2[:]))
-            return by_key, by_query
 
-        def quantise_a2(h, by_key, by_query):
+        def flip_a2(h, a2):
+            by_key = soft.tile([P, PACK, P, PACK], BF16, align_bytes=64)
+            a2_words = a2[:].bitcast(F32).rearrange("m j (p u) -> m j u p", u=2)
+            for pair in range(0, PACK, 2):
+                flipped = work.tile([P, 2, 2, P], F32, tag="flip")
+                for a in range(2):
+                    for u in range(2):
+                        nc.tensor.transpose(flipped[:, a, u, :], a2_words[:, pair + a, u, :], ident_words[:])
+                nc.scalar.copy(
+                    out=by_key[:, pair : pair + 2, :, :].bitcast(F32),
+                    in_=flipped[:].rearrange("p a u m -> p a m u"),
+                )
+            by_key_of[h] = by_key
+
+        def regroup_a2(a2):
+            by_query = soft.tile([P, TOKENS, PACK], BF16, align_bytes=64)
+            nc.vector.tensor_copy(
+                out=by_query[:].rearrange("p (i m) t -> p m t i", i=PACK),
+                in_=a2[:].rearrange("p t (m i) -> p m t i", i=PACK),
+            )
+            return by_query
+
+        def quantise_by_query(h, by_query):
             quantise(
                 by_query[:].rearrange("p c t -> p (c t)"),
                 by_query_codes[:, h, :],
                 by_query_scales[:, h, :],
             )
+
+        def quantise_by_key(h):
             quantise(
-                by_key[:].rearrange("p j m t -> p (j m t)"),
+                by_key_of.pop(h)[:].rearrange("p j m t -> p (j m t)"),
                 by_key_codes[:, h, :],
                 by_key_scales[:, h, :],
             )
@@ -245,35 +261,54 @@ def tile_multiheadattention_pa_kernel(tc, K, Q, F1, F2, out):
         acc_hi = []
 
         for t in range(len(steps) + 2):
+            scoring = t < HEADS
+            finishing = 1 <= t <= HEADS
             if t + AHEAD < len(steps):
                 load_step(t + AHEAD)
+            if t < len(steps):
+                regroup_f2(t)
+            if finishing:
+                inverse, a2 = invert_sums(t - 1)
+            if scoring:
+                shifted(t, 0)
+                score(t, 2)
+                shifted(t, 1)
+                score(t, 3)
             if t + 1 < HEADS:
                 flip_qk(t + 1)
-            if t < HEADS:
-                exponential(t, 0)
-                score(t, 2)
-                exponential(t, 1)
-                score(t, 3)
-                exponential(t, 2)
-                exponential(t, 3)
-            if t + 1 < HEADS:
                 copy_qk(t + 1)
-            if 1 <= t <= HEADS:
-                by_key, by_query = normalise_and_flip(t - 1)
+            if 2 <= t <= HEADS + 1:
+                quantise_by_key(t - 2)
+            if scoring:
+                shifted(t, 2)
+            if 1 <= t <= len(steps):
+                quantise_f(t - 1, 1)
+            if scoring:
+                shifted(t, 3)
+            if 1 <= t <= len(steps):
+                quantise_f(t - 1, 2)
             if t == HEADS + 2:
                 acc_hi.extend(work.tile([P, HALF], F32, tag="score", name="acc_hi%d" % i) for i in range(2))
                 acc_hi.extend(work.tile([P, HALF], F32, tag="flip", name="acc_hi%d" % i) for i in range(2, 4))
             if 2 <= t:
                 multiply_step(t - 2, acc_lo if t - 2 < HEADS else acc_hi)
+            if finishing:
+                for j in range(PACK):
+                    normalise(t - 1, j, inverse, a2)
+            if scoring:
+                for j in range(PACK):
+                    exponential(t, j)
+            if finishing:
+                flip_a2(t - 1, a2)
             if t + 1 < HEADS:
                 score(t + 1, 0)
                 score(t + 1, 1)
-            if 1 <= t <= len(steps):
-                quantise_step(t - 1)
+            if finishing:
+                by_query = regroup_a2(a2)
             if t < len(steps):
-                regroup_step(t)
-            if 1 <= t <= HEADS:
-                quantise_a2(t - 1, by_key, by_query)
+                regroup_f1(t)
+            if finishing:
+                quantise_by_query(t - 1, by_query)
             if t - 2 == HEADS - 1:
                 store_half(0, acc_lo)
         store_half(1, acc_hi)

@@ -18,11 +18,10 @@ HEADS = 8
 Z = 128
 D = 1024
 HALF = 512
-HALVES = D // HALF
 BETA = 1.0 / (Z**0.5)
 RUN = 4
-HEAD_CUTS = (0, 1, 4, 8)
-AHEAD = 9
+STEPS = 2 * HEADS
+AHEAD = 8
 
 FLOPS = 2 * HEADS * TOKENS * TOKENS * Z + 2 * 2 * HEADS * TOKENS * TOKENS * D
 
@@ -38,30 +37,25 @@ def rows_first(raw):
 def tile_multiheadattention_pa_kernel(tc, K, Q, F1, F2, out):
     nc = tc.nc
 
-    q_rows = Q.rearrange("(p j) h z -> p j h z", j=PACK)
+    q_rows = Q.rearrange("(j p) h z -> p j h z", p=P)
     k_rows = K.rearrange("(j p) h z -> p j h z", p=P)
     f1_rows = F1.rearrange("(p j) h d -> p j h d", j=PACK)
-    f2_rows = F2.rearrange("(p j) h d -> p j h d", j=PACK)
-    out_rows = out.rearrange("(p j) d -> p j d", j=PACK)
-
-    steps = [(half, h) for half in range(HALVES) for h in range(HEADS)]
+    f2_rows = F2.rearrange("(j p) h d -> p j h d", p=P)
+    out_rows = out.rearrange("(j p) d -> p j d", p=P)
 
     with ExitStack() as ctx:
         ctx.enter_context(tc.manual_schedule())
         keep = ctx.enter_context(tc.tile_pool(name="keep", bufs=1))
         raw_pool = ctx.enter_context(tc.tile_pool(name="raw", bufs=AHEAD + 1))
         soft = ctx.enter_context(tc.tile_pool(name="soft", bufs=2))
-        stage = ctx.enter_context(tc.tile_pool(name="stage", bufs=3))
+        grouped_pool = ctx.enter_context(tc.tile_pool(name="grouped", bufs=2))
+        codes_pool = ctx.enter_context(tc.tile_pool(name="codes", bufs=4))
         results = ctx.enter_context(tc.tile_pool(name="results", bufs=PACK))
         acc_pool = ctx.enter_context(tc.psum_pool(name="acc", bufs=1))
         work = ctx.enter_context(tc.psum_pool(name="work", bufs=2))
 
         q_raw = keep.tile([P, PACK, HEADS, Z], BF16)
         k_raw = keep.tile([P, PACK, HEADS, Z], BF16)
-        for first, last in zip(HEAD_CUTS[:-1], HEAD_CUTS[1:]):
-            nc.sync.dma_start(out=k_raw[:, :, first:last, :], in_=k_rows[:, :, first:last, :])
-            nc.sync.dma_start(out=q_raw[:, :, first:last, :], in_=q_rows[:, :, first:last, :])
-
         ident = keep.tile([P, P], BF16)
         make_identity(nc, ident[:])
         ident_words = keep.tile([P, P], F32)
@@ -72,6 +66,9 @@ def tile_multiheadattention_pa_kernel(tc, K, Q, F1, F2, out):
         by_query_codes = keep.tile([P, HEADS, TOKENS], U32, align_bytes=64)
         by_query_scales = keep.tile([P, HEADS, TOKENS], U8, align_bytes=64)
 
+        acc_lo = [acc_pool.tile([P, HALF], F32, name="acc_lo%d" % i) for i in range(PACK)]
+        acc_hi = []
+
         f_raw = {}
         f_grouped = {}
         f_quantised = {}
@@ -81,14 +78,22 @@ def tile_multiheadattention_pa_kernel(tc, K, Q, F1, F2, out):
         expo = {}
         shift = {}
         sums = {}
-        by_key_of = {}
+        inverse = {}
+        a2 = {}
+        flipped_a2 = {}
+        by_key = {}
+        by_query = {}
 
         def quantise(grouped, codes, scales):
             nc.vector.quantize_mx(out=codes.bitcast(FP8X4), scales=scales, in_=grouped)
 
-        def load_step(s):
-            half, h = steps[s]
-            cols = slice(half * HALF, (half + 1) * HALF)
+        def load_qk(first, last):
+            nc.sync.dma_start(out=k_raw[:, :, first:last, :], in_=k_rows[:, :, first:last, :])
+            nc.sync.dma_start(out=q_raw[:, :, first:last, :], in_=q_rows[:, :, first:last, :])
+
+        def load_f(s):
+            h = s % HEADS
+            cols = slice((s // HEADS) * HALF, (s // HEADS + 1) * HALF)
             f1_raw = raw_pool.tile([P, PACK, HALF], BF16)
             nc.sync.dma_start(out=f1_raw[:], in_=f1_rows[:, :, h, cols])
             f2_raw = raw_pool.tile([P, PACK, HALF], BF16)
@@ -96,48 +101,51 @@ def tile_multiheadattention_pa_kernel(tc, K, Q, F1, F2, out):
             f_raw[s] = (f1_raw, f2_raw)
 
         def regroup_f2(s):
-            f2_grouped = stage.tile([P, HALF, PACK], BF16, align_bytes=64)
+            f2_grouped = grouped_pool.tile([P, HALF, PACK], BF16, align_bytes=64)
             nc.scalar.copy(out=words_first(f2_grouped[:]), in_=rows_first(f_raw[s][1][:]))
             f_grouped[(s, 2)] = f2_grouped
 
         def regroup_f1(s):
-            f1_grouped = stage.tile([P, HALF, PACK], BF16, align_bytes=64)
+            f1_grouped = grouped_pool.tile([P, HALF, PACK], BF16, align_bytes=64)
             nc.vector.tensor_copy(out=words_first(f1_grouped[:]), in_=rows_first(f_raw.pop(s)[0][:]))
             f_grouped[(s, 1)] = f1_grouped
 
         def quantise_f(s, which):
-            codes = stage.tile([P, HALF], U32, align_bytes=64, name="f%d_codes" % which)
-            scales = stage.tile([P, HALF], U8, align_bytes=64, name="f%d_scales" % which)
+            codes = codes_pool.tile([P, HALF], U32, align_bytes=64, name="f%d_codes" % which)
+            scales = codes_pool.tile([P, HALF], U8, align_bytes=64, name="f%d_scales" % which)
             quantise(f_grouped.pop((s, which))[:].rearrange("p c t -> p (c t)"), codes[:], scales[:])
             f_quantised[(s, which)] = (codes, scales)
 
-        def multiply_step(s, acc):
-            h = steps[s][1]
-            f1_codes, f1_scales = f_quantised.pop((s, 1))
-            f2_codes, f2_scales = f_quantised.pop((s, 2))
+        def banks_of(s):
+            if s < HEADS:
+                return acc_lo
+            if not acc_hi:
+                acc_hi.extend(work.tile([P, HALF], F32, tag="score", name="acc_hi%d" % i) for i in range(2))
+                acc_hi.extend(work.tile([P, HALF], F32, tag="flip", name="acc_hi%d" % i) for i in range(2, 4))
+            return acc_hi
+
+        def multiply(s, which):
+            h = s % HEADS
+            acc = banks_of(s)
+            a2_codes, a2_scales = (by_key_codes, by_key_scales) if which == 1 else (by_query_codes, by_query_scales)
+            f_codes, f_scales = f_quantised.pop((s, which))
             for i in range(PACK):
                 rows = slice(i * P, (i + 1) * P)
                 nc.tensor.matmul_mx(
                     out=acc[i][:],
-                    lhsT=by_key_codes[:, h, rows].bitcast(FP8X4),
-                    lhsT_scale=by_key_scales[:, h, rows],
-                    rhs=f1_codes[:].bitcast(FP8X4),
-                    rhs_scale=f1_scales[:],
-                    start=(h == 0),
-                    stop=False,
-                )
-                nc.tensor.matmul_mx(
-                    out=acc[i][:],
-                    lhsT=by_query_codes[:, h, rows].bitcast(FP8X4),
-                    lhsT_scale=by_query_scales[:, h, rows],
-                    rhs=f2_codes[:].bitcast(FP8X4),
-                    rhs_scale=f2_scales[:],
-                    start=False,
-                    stop=(h == HEADS - 1),
+                    lhsT=a2_codes[:, h, rows].bitcast(FP8X4),
+                    lhsT_scale=a2_scales[:, h, rows],
+                    rhs=f_codes[:].bitcast(FP8X4),
+                    rhs_scale=f_scales[:],
+                    start=(h == 0 and which == 1),
+                    stop=(h == HEADS - 1 and which == 2),
                 )
 
-        def store_half(half, acc):
-            cols = slice(half * HALF, (half + 1) * HALF)
+        def store_half(s):
+            if s % HEADS != HEADS - 1:
+                return
+            acc = banks_of(s)
+            cols = slice((s // HEADS) * HALF, (s // HEADS + 1) * HALF)
             for i in range(PACK):
                 result = results.tile([P, HALF], F32)
                 if i % 2 == 0:
@@ -163,7 +171,7 @@ def tile_multiheadattention_pa_kernel(tc, K, Q, F1, F2, out):
             nc.tensor.matmul(
                 out=bank[:],
                 lhsT=qk_t[h][:, 0, j, :],
-                rhs=qk_t[h][:, 1, :, :].rearrange("z j m -> z (j m)"),
+                rhs=qk_t[h][:, 1, :, :].rearrange("z j p -> z (j p)"),
                 start=True,
                 stop=True,
             )
@@ -195,120 +203,105 @@ def tile_multiheadattention_pa_kernel(tc, K, Q, F1, F2, out):
             )
 
         def invert_sums(h):
-            inverse = soft.tile([P, PACK], F32)
-            nc.vector.reciprocal(out=inverse[:], in_=sums.pop(h)[:])
-            a2 = soft.tile([P, PACK, TOKENS], BF16)
-            return inverse, a2
+            inverse[h] = soft.tile([P, PACK], F32, name="inverse")
+            nc.vector.reciprocal(out=inverse[h][:], in_=sums[h][:])
+            a2[h] = soft.tile([P, PACK, TOKENS], BF16, name="a2")
 
-        def normalise(h, j, inverse, a2):
+        def normalise(h, j):
             if j < PACK // 2:
                 nc.vector.tensor_scalar(
-                    out=a2[:, j, :],
+                    out=a2[h][:, j, :],
                     in0=expo[h][:, j, :],
-                    scalar1=inverse[:, j : j + 1],
+                    scalar1=inverse[h][:, j : j + 1],
                     scalar2=None,
                     op0=ALU.mult,
                 )
             else:
                 nc.scalar.activation(
-                    out=a2[:, j, :], in_=expo[h][:, j, :], func=ACT.Copy, scale=inverse[:, j : j + 1]
+                    out=a2[h][:, j, :], in_=expo[h][:, j, :], func=ACT.Copy, scale=inverse[h][:, j : j + 1]
                 )
 
-        def flip_a2(h, a2):
-            by_key = soft.tile([P, PACK, P, PACK], BF16, align_bytes=64)
-            a2_words = a2[:].bitcast(F32).rearrange("m j (p u) -> m j u p", u=2)
-            for pair in range(0, PACK, 2):
-                flipped = work.tile([P, 2, 2, P], F32, tag="flip")
-                for a in range(2):
-                    for u in range(2):
-                        nc.tensor.transpose(flipped[:, a, u, :], a2_words[:, pair + a, u, :], ident_words[:])
-                nc.scalar.copy(
-                    out=by_key[:, pair : pair + 2, :, :].bitcast(F32),
-                    in_=flipped[:].rearrange("p a u m -> p a m u"),
-                )
-            by_key_of[h] = by_key
+        def flip_a2(h, pair):
+            a2_words = a2[h][:].bitcast(F32).rearrange("m j (p u) -> m j u p", u=2)
+            flipped = work.tile([P, 2, 2, P], F32, tag="flip")
+            for a in range(2):
+                for u in range(2):
+                    nc.tensor.transpose(flipped[:, a, u, :], a2_words[:, pair + a, u, :], ident_words[:])
+            flipped_a2[(h, pair)] = flipped
 
-        def regroup_a2(a2):
-            by_query = soft.tile([P, TOKENS, PACK], BF16, align_bytes=64)
-            nc.vector.tensor_copy(
-                out=by_query[:].rearrange("p (i m) t -> p m t i", i=PACK),
-                in_=a2[:].rearrange("p t (m i) -> p m t i", i=PACK),
+        def copy_by_key(h, pair):
+            if pair == 0:
+                by_key[h] = soft.tile([P, PACK, P, PACK], BF16, align_bytes=64, name="by_key")
+            nc.scalar.copy(
+                out=by_key[h][:, pair : pair + 2, :, :].bitcast(F32),
+                in_=flipped_a2.pop((h, pair))[:].rearrange("p a u m -> p a m u"),
             )
-            return by_query
 
-        def quantise_by_query(h, by_query):
+        def regroup_by_query(h):
+            by_query[h] = soft.tile([P, TOKENS, PACK], BF16, align_bytes=64, name="by_query")
+            nc.vector.tensor_copy(out=words_first(by_query[h][:]), in_=rows_first(a2[h][:]))
+
+        def quantise_by_query(h):
             quantise(
-                by_query[:].rearrange("p c t -> p (c t)"),
+                by_query.pop(h)[:].rearrange("p c t -> p (c t)"),
                 by_query_codes[:, h, :],
                 by_query_scales[:, h, :],
             )
 
         def quantise_by_key(h):
             quantise(
-                by_key_of.pop(h)[:].rearrange("p j m t -> p (j m t)"),
+                by_key.pop(h)[:].rearrange("p j m t -> p (j m t)"),
                 by_key_codes[:, h, :],
                 by_key_scales[:, h, :],
             )
 
-        for s in range(AHEAD):
-            load_step(s)
-        flip_qk(0)
-        copy_qk(0)
-        score(0, 0)
-        score(0, 1)
+        def for_head(h, action, *args):
+            if 0 <= h < HEADS:
+                action(h, *args)
 
-        acc_lo = [acc_pool.tile([P, HALF], F32, name="acc_lo%d" % i) for i in range(PACK)]
-        acc_hi = []
+        def for_step(s, action, *args):
+            if 0 <= s < STEPS:
+                action(s, *args)
 
-        for t in range(len(steps) + 2):
-            scoring = t < HEADS
-            finishing = 1 <= t <= HEADS
-            if t + AHEAD < len(steps):
-                load_step(t + AHEAD)
-            if t < len(steps):
-                regroup_f2(t)
-            if finishing:
-                inverse, a2 = invert_sums(t - 1)
-            if scoring:
-                shifted(t, 0)
-                score(t, 2)
-                shifted(t, 1)
-                score(t, 3)
-            if t + 1 < HEADS:
-                flip_qk(t + 1)
-                copy_qk(t + 1)
-            if 2 <= t <= HEADS + 1:
-                quantise_by_key(t - 2)
-            if scoring:
-                shifted(t, 2)
-            if 1 <= t <= len(steps):
-                quantise_f(t - 1, 1)
-            if scoring:
-                shifted(t, 3)
-            if 1 <= t <= len(steps):
-                quantise_f(t - 1, 2)
-            if t == HEADS + 2:
-                acc_hi.extend(work.tile([P, HALF], F32, tag="score", name="acc_hi%d" % i) for i in range(2))
-                acc_hi.extend(work.tile([P, HALF], F32, tag="flip", name="acc_hi%d" % i) for i in range(2, 4))
-            if 2 <= t:
-                multiply_step(t - 2, acc_lo if t - 2 < HEADS else acc_hi)
-            if finishing:
-                for j in range(PACK):
-                    normalise(t - 1, j, inverse, a2)
-            if scoring:
-                for j in range(PACK):
-                    exponential(t, j)
-            if finishing:
-                flip_a2(t - 1, a2)
-            if t + 1 < HEADS:
-                score(t + 1, 0)
-                score(t + 1, 1)
-            if finishing:
-                by_query = regroup_a2(a2)
-            if t < len(steps):
-                regroup_f1(t)
-            if finishing:
-                quantise_by_query(t - 1, by_query)
-            if t - 2 == HEADS - 1:
-                store_half(0, acc_lo)
-        store_half(1, acc_hi)
+        load_qk(0, 1)
+        load_qk(1, HEADS // 2)
+        load_f(0)
+        load_qk(HEADS // 2, HEADS)
+        for s in range(1, AHEAD - 1):
+            load_f(s)
+
+        for t in range(-1, STEPS + 5):
+            for_step(t + AHEAD, load_f)
+            for_head(t - 2, copy_by_key, 0)
+            for_head(t - 2, copy_by_key, 2)
+            for_head(t - 1, invert_sums)
+            for_head(t - 1, normalise, 0)
+            for_head(t - 1, normalise, 1)
+            for_head(t, shifted, 0)
+            for_head(t, score, 2)
+            for_head(t, exponential, 0)
+            for_head(t, shifted, 1)
+            for_head(t, score, 3)
+            for_head(t, exponential, 1)
+            for_head(t + 1, flip_qk)
+            for_step(t - 3, multiply, 1)
+            for_head(t - 2, quantise_by_query)
+            for_head(t - 1, normalise, 2)
+            for_head(t, shifted, 2)
+            for_head(t, exponential, 2)
+            for_head(t + 1, copy_qk)
+            for_head(t - 2, quantise_by_key)
+            for_head(t - 1, normalise, 3)
+            for_head(t, shifted, 3)
+            for_head(t, exponential, 3)
+            for_head(t + 1, score, 0)
+            for_head(t + 1, score, 1)
+            for_head(t - 1, flip_a2, 0)
+            for_head(t - 1, flip_a2, 2)
+            for_step(t - 3, multiply, 2)
+            for_step(t - 1, quantise_f, 1)
+            for_step(t - 1, quantise_f, 2)
+            for_step(t, regroup_f2)
+            for_step(t, regroup_f1)
+            for_head(t - 1, regroup_by_query)
+            for_step(t - 4, store_half)

@@ -94,10 +94,10 @@ def tile_multiheadattention_pa_kernel(tc, K, Q, F1, F2, out):
         def load_f(s):
             h = s % HEADS
             cols = slice((s // HEADS) * HALF, (s // HEADS + 1) * HALF)
-            f1_raw = raw_pool.tile([P, PACK, HALF], BF16)
-            nc.sync.dma_start(out=f1_raw[:], in_=f1_rows[:, :, h, cols])
             f2_raw = raw_pool.tile([P, PACK, HALF], BF16)
             nc.sync.dma_start(out=f2_raw[:], in_=f2_rows[:, :, h, cols])
+            f1_raw = raw_pool.tile([P, PACK, HALF], BF16)
+            nc.sync.dma_start(out=f1_raw[:], in_=f1_rows[:, :, h, cols])
             f_raw[s] = (f1_raw, f2_raw)
 
         def regroup_f2(s):
@@ -263,18 +263,23 @@ def tile_multiheadattention_pa_kernel(tc, K, Q, F1, F2, out):
             if 0 <= s < STEPS:
                 action(s, *args)
 
+        def step_of(t):
+            if t + 1 < HEADS:
+                return t + 1
+            return t if t >= HEADS else -1
+
         load_qk(0, 1)
-        load_qk(1, HEADS // 2)
         load_f(0)
+        load_qk(1, HEADS // 2)
+        load_f(1)
         load_qk(HEADS // 2, HEADS)
-        for s in range(1, AHEAD - 1):
+        for s in range(2, AHEAD - 1):
             load_f(s)
 
         for t in range(-1, STEPS + 5):
             for_step(t + AHEAD, load_f)
             for_head(t - 2, copy_by_key, 0)
             for_head(t - 2, copy_by_key, 2)
-            for_head(t - 1, invert_sums)
             for_head(t - 1, normalise, 0)
             for_head(t - 1, normalise, 1)
             for_head(t, shifted, 0)
@@ -299,9 +304,10 @@ def tile_multiheadattention_pa_kernel(tc, K, Q, F1, F2, out):
             for_head(t - 1, flip_a2, 0)
             for_head(t - 1, flip_a2, 2)
             for_step(t - 3, multiply, 2)
-            for_step(t - 1, quantise_f, 1)
-            for_step(t - 1, quantise_f, 2)
-            for_step(t, regroup_f2)
-            for_step(t, regroup_f1)
+            for_step(step_of(t - 1), quantise_f, 1)
+            for_step(step_of(t - 1), quantise_f, 2)
+            for_step(step_of(t), regroup_f2)
+            for_step(step_of(t), regroup_f1)
+            for_head(t, invert_sums)
             for_head(t - 1, regroup_by_query)
             for_step(t - 4, store_half)

@@ -208,18 +208,14 @@ def tile_multiheadattention_pa_kernel(tc, K, Q, F1, F2, out):
             a2[h] = soft.tile([P, PACK, TOKENS], BF16, name="a2")
 
         def normalise(h, j):
-            if j < PACK // 2:
-                nc.vector.tensor_scalar(
-                    out=a2[h][:, j, :],
-                    in0=expo[h][:, j, :],
-                    scalar1=inverse[h][:, j : j + 1],
-                    scalar2=None,
-                    op0=ALU.mult,
-                )
-            else:
-                nc.scalar.activation(
-                    out=a2[h][:, j, :], in_=expo[h][:, j, :], func=ACT.Copy, scale=inverse[h][:, j : j + 1]
-                )
+            nc.gpsimd.tensor_scalar(
+                out=a2[h][:, j, :],
+                in0=expo[h][:, j, :],
+                scalar1=inverse[h][:, j : j + 1],
+                scalar2=0.0,
+                op0=ALU.mult,
+                op1=ALU.add,
+            )
 
         def flip_a2(h, pair):
             a2_words = a2[h][:].bitcast(F32).rearrange("m j (p u) -> m j u p", u=2)
@@ -278,27 +274,26 @@ def tile_multiheadattention_pa_kernel(tc, K, Q, F1, F2, out):
 
         for t in range(-1, STEPS + 5):
             for_step(t + AHEAD, load_f)
+            for_head(t - 1, invert_sums)
+            for j in range(PACK):
+                for_head(t - 1, normalise, j)
             for_head(t - 2, copy_by_key, 0)
             for_head(t - 2, copy_by_key, 2)
-            for_head(t - 1, normalise, 0)
-            for_head(t - 1, normalise, 1)
             for_head(t, shifted, 0)
             for_head(t, score, 2)
             for_head(t, exponential, 0)
             for_head(t, shifted, 1)
             for_head(t, score, 3)
             for_head(t, exponential, 1)
-            for_head(t + 1, flip_qk)
-            for_step(t - 3, multiply, 1)
-            for_head(t - 2, quantise_by_query)
-            for_head(t - 1, normalise, 2)
             for_head(t, shifted, 2)
             for_head(t, exponential, 2)
-            for_head(t + 1, copy_qk)
-            for_head(t - 2, quantise_by_key)
-            for_head(t - 1, normalise, 3)
             for_head(t, shifted, 3)
             for_head(t, exponential, 3)
+            for_head(t + 1, flip_qk)
+            for_step(t - 3, multiply, 1)
+            for_head(t + 1, copy_qk)
+            for_head(t - 2, quantise_by_query)
+            for_head(t - 2, quantise_by_key)
             for_head(t + 1, score, 0)
             for_head(t + 1, score, 1)
             for_head(t - 1, flip_a2, 0)
@@ -308,6 +303,5 @@ def tile_multiheadattention_pa_kernel(tc, K, Q, F1, F2, out):
             for_step(step_of(t - 1), quantise_f, 2)
             for_step(step_of(t), regroup_f2)
             for_step(step_of(t), regroup_f1)
-            for_head(t, invert_sums)
             for_head(t - 1, regroup_by_query)
             for_step(t - 4, store_half)

@@ -22,6 +22,7 @@ BETA = 1.0 / (Z**0.5)
 RUN = 4
 STEPS = 2 * HEADS
 AHEAD = 8
+F1_SHARE = 256
 
 FLOPS = 2 * HEADS * TOKENS * TOKENS * Z + 2 * 2 * HEADS * TOKENS * TOKENS * D
 
@@ -52,7 +53,7 @@ def tile_multiheadattention_pa_kernel(tc, K, Q, F1, F2, out):
         codes_pool = ctx.enter_context(tc.tile_pool(name="codes", bufs=4))
         results = ctx.enter_context(tc.tile_pool(name="results", bufs=PACK))
         acc_pool = ctx.enter_context(tc.psum_pool(name="acc", bufs=1))
-        work = ctx.enter_context(tc.psum_pool(name="work", bufs=2))
+        work = ctx.enter_context(tc.psum_pool(name="work", bufs=PACK))
 
         q_raw = keep.tile([P, PACK, HEADS, Z], BF16)
         k_raw = keep.tile([P, PACK, HEADS, Z], BF16)
@@ -100,15 +101,26 @@ def tile_multiheadattention_pa_kernel(tc, K, Q, F1, F2, out):
             nc.sync.dma_start(out=f1_raw[:], in_=f1_rows[:, :, h, cols])
             f_raw[s] = (f1_raw, f2_raw)
 
+        def scalar_share(s):
+            return F1_SHARE if s < HEADS else 0
+
         def regroup_f2(s):
             f2_grouped = grouped_pool.tile([P, HALF, PACK], BF16, align_bytes=64)
             nc.scalar.copy(out=words_first(f2_grouped[:]), in_=rows_first(f_raw[s][1][:]))
             f_grouped[(s, 2)] = f2_grouped
+            f1_grouped = grouped_pool.tile([P, HALF, PACK], BF16, align_bytes=64)
+            f_grouped[(s, 1)] = f1_grouped
+            share = scalar_share(s)
+            if share:
+                nc.scalar.copy(
+                    out=words_first(f1_grouped[:, :share, :]), in_=rows_first(f_raw[s][0][:, :, :share])
+                )
 
         def regroup_f1(s):
-            f1_grouped = grouped_pool.tile([P, HALF, PACK], BF16, align_bytes=64)
-            nc.vector.tensor_copy(out=words_first(f1_grouped[:]), in_=rows_first(f_raw.pop(s)[0][:]))
-            f_grouped[(s, 1)] = f1_grouped
+            share = scalar_share(s)
+            nc.vector.tensor_copy(
+                out=words_first(f_grouped[(s, 1)][:, share:, :]), in_=rows_first(f_raw.pop(s)[0][:, :, share:])
+            )
 
         def quantise_f(s, which):
             codes = codes_pool.tile([P, HALF], U32, align_bytes=64, name="f%d_codes" % which)
@@ -120,8 +132,7 @@ def tile_multiheadattention_pa_kernel(tc, K, Q, F1, F2, out):
             if s < HEADS:
                 return acc_lo
             if not acc_hi:
-                acc_hi.extend(work.tile([P, HALF], F32, tag="score", name="acc_hi%d" % i) for i in range(2))
-                acc_hi.extend(work.tile([P, HALF], F32, tag="flip", name="acc_hi%d" % i) for i in range(2, 4))
+                acc_hi.extend(work.tile([P, HALF], F32, tag="work", name="acc_hi%d" % i) for i in range(PACK))
             return acc_hi
 
         def multiply(s, which):
@@ -155,7 +166,7 @@ def tile_multiheadattention_pa_kernel(tc, K, Q, F1, F2, out):
                 nc.sync.dma_start(out=out_rows[:, i, cols], in_=result[:])
 
         def flip_qk(h):
-            flipped = work.tile([P, 2, PACK, P], BF16, tag="flip")
+            flipped = work.tile([P, 2, PACK, P], BF16, tag="work")
             for j in range(PACK):
                 nc.tensor.transpose(flipped[:, 0, j, :], q_raw[:, j, h, :], ident[:])
                 nc.tensor.transpose(flipped[:, 1, j, :], k_raw[:, j, h, :], ident[:])
@@ -167,7 +178,7 @@ def tile_multiheadattention_pa_kernel(tc, K, Q, F1, F2, out):
             qk_t[h] = qk
 
         def score(h, j):
-            bank = work.tile([P, TOKENS], F32, tag="score")
+            bank = work.tile([P, TOKENS], F32, tag="work")
             nc.tensor.matmul(
                 out=bank[:],
                 lhsT=qk_t[h][:, 0, j, :],
@@ -208,25 +219,34 @@ def tile_multiheadattention_pa_kernel(tc, K, Q, F1, F2, out):
             a2[h] = soft.tile([P, PACK, TOKENS], BF16, name="a2")
 
         def normalise(h, j):
-            nc.gpsimd.tensor_scalar(
-                out=a2[h][:, j, :],
-                in0=expo[h][:, j, :],
-                scalar1=inverse[h][:, j : j + 1],
-                scalar2=0.0,
-                op0=ALU.mult,
-                op1=ALU.add,
-            )
+            if j < PACK // 2:
+                nc.vector.tensor_scalar(
+                    out=a2[h][:, j, :],
+                    in0=expo[h][:, j, :],
+                    scalar1=inverse[h][:, j : j + 1],
+                    scalar2=None,
+                    op0=ALU.mult,
+                )
+            else:
+                nc.gpsimd.tensor_scalar(
+                    out=a2[h][:, j, :],
+                    in0=expo[h][:, j, :],
+                    scalar1=inverse[h][:, j : j + 1],
+                    scalar2=0.0,
+                    op0=ALU.mult,
+                    op1=ALU.add,
+                )
 
         def flip_a2(h, pair):
             a2_words = a2[h][:].bitcast(F32).rearrange("m j (p u) -> m j u p", u=2)
-            flipped = work.tile([P, 2, 2, P], F32, tag="flip")
+            flipped = work.tile([P, 2, 2, P], F32, tag="work")
             for a in range(2):
                 for u in range(2):
                     nc.tensor.transpose(flipped[:, a, u, :], a2_words[:, pair + a, u, :], ident_words[:])
             flipped_a2[(h, pair)] = flipped
 
         def copy_by_key(h, pair):
-            if pair == 0:
+            if h not in by_key:
                 by_key[h] = soft.tile([P, PACK, P, PACK], BF16, align_bytes=64, name="by_key")
             nc.scalar.copy(
                 out=by_key[h][:, pair : pair + 2, :, :].bitcast(F32),
@@ -275,30 +295,25 @@ def tile_multiheadattention_pa_kernel(tc, K, Q, F1, F2, out):
         for t in range(-1, STEPS + 5):
             for_step(t + AHEAD, load_f)
             for_head(t - 1, invert_sums)
+            for_head(t - 1, normalise, 2)
+            for_head(t - 1, normalise, 3)
             for j in range(PACK):
-                for_head(t - 1, normalise, j)
-            for_head(t - 2, copy_by_key, 0)
-            for_head(t - 2, copy_by_key, 2)
-            for_head(t, shifted, 0)
-            for_head(t, score, 2)
-            for_head(t, exponential, 0)
-            for_head(t, shifted, 1)
-            for_head(t, score, 3)
-            for_head(t, exponential, 1)
-            for_head(t, shifted, 2)
-            for_head(t, exponential, 2)
-            for_head(t, shifted, 3)
-            for_head(t, exponential, 3)
+                for_head(t, shifted, j)
+                for_head(t, exponential, j)
+            for_head(t - 1, normalise, 0)
+            for_head(t - 1, normalise, 1)
             for_head(t + 1, flip_qk)
             for_step(t - 3, multiply, 1)
             for_head(t + 1, copy_qk)
+            for_head(t - 1, flip_a2, 2)
+            for_head(t - 1, flip_a2, 0)
+            for_head(t - 1, copy_by_key, 2)
+            for_head(t - 1, copy_by_key, 0)
             for_head(t - 2, quantise_by_query)
             for_head(t - 2, quantise_by_key)
-            for_head(t + 1, score, 0)
-            for_head(t + 1, score, 1)
-            for_head(t - 1, flip_a2, 0)
-            for_head(t - 1, flip_a2, 2)
             for_step(t - 3, multiply, 2)
+            for j in range(PACK):
+                for_head(t + 1, score, j)
             for_step(step_of(t - 1), quantise_f, 1)
             for_step(step_of(t - 1), quantise_f, 2)
             for_step(step_of(t), regroup_f2)

@@ -22,7 +22,7 @@ BETA = 1.0 / (Z**0.5)
 RUN = 4
 STEPS = 2 * HEADS
 AHEAD = 8
-F1_SHARE = 256
+F1_SHARE = 128
 
 FLOPS = 2 * HEADS * TOKENS * TOKENS * Z + 2 * 2 * HEADS * TOKENS * TOKENS * D
 

@@ -22,7 +22,8 @@ BETA = 1.0 / (Z**0.5)
 RUN = 4
 STEPS = 2 * HEADS
 AHEAD = 8
-F1_SHARE = 128
+G_COLS = 384
+S_COLS = 64
 
 FLOPS = 2 * HEADS * TOKENS * TOKENS * Z + 2 * 2 * HEADS * TOKENS * TOKENS * D
 
@@ -50,7 +51,8 @@ def tile_multiheadattention_pa_kernel(tc, K, Q, F1, F2, out):
         raw_pool = ctx.enter_context(tc.tile_pool(name="raw", bufs=AHEAD + 1))
         soft = ctx.enter_context(tc.tile_pool(name="soft", bufs=2))
         grouped_pool = ctx.enter_context(tc.tile_pool(name="grouped", bufs=2))
-        codes_pool = ctx.enter_context(tc.tile_pool(name="codes", bufs=4))
+        single_pool = ctx.enter_context(tc.tile_pool(name="single", bufs=1))
+        codes_pool = ctx.enter_context(tc.tile_pool(name="codes", bufs=5))
         results = ctx.enter_context(tc.tile_pool(name="results", bufs=PACK))
         acc_pool = ctx.enter_context(tc.psum_pool(name="acc", bufs=1))
         work = ctx.enter_context(tc.psum_pool(name="work", bufs=PACK))
@@ -101,25 +103,39 @@ def tile_multiheadattention_pa_kernel(tc, K, Q, F1, F2, out):
             nc.sync.dma_start(out=f1_raw[:], in_=f1_rows[:, :, h, cols])
             f_raw[s] = (f1_raw, f2_raw)
 
-        def scalar_share(s):
-            return F1_SHARE if s < HEADS else 0
+        def beside_scores(s):
+            return 1 <= s <= HEADS
 
-        def regroup_f2(s):
-            f2_grouped = grouped_pool.tile([P, HALF, PACK], BF16, align_bytes=64)
-            nc.scalar.copy(out=words_first(f2_grouped[:]), in_=rows_first(f_raw[s][1][:]))
-            f_grouped[(s, 2)] = f2_grouped
-            f1_grouped = grouped_pool.tile([P, HALF, PACK], BF16, align_bytes=64)
-            f_grouped[(s, 1)] = f1_grouped
-            share = scalar_share(s)
-            if share:
-                nc.scalar.copy(
-                    out=words_first(f1_grouped[:, :share, :]), in_=rows_first(f_raw[s][0][:, :, :share])
+        def open_step(s):
+            pool = single_pool if beside_scores(s) else grouped_pool
+            f_grouped[(s, 2)] = pool.tile([P, HALF, PACK], BF16, align_bytes=64, name="f2_grouped")
+            f_grouped[(s, 1)] = grouped_pool.tile([P, HALF, PACK], BF16, align_bytes=64, name="f1_grouped")
+
+        def regroup_gpsimd(s):
+            if beside_scores(s):
+                nc.gpsimd.tensor_scalar(
+                    out=f_grouped[(s, 2)][:, :G_COLS, :],
+                    in0=f_raw[s][1][:, :, :G_COLS].rearrange("p t c -> p c t"),
+                    scalar1=1.0,
+                    scalar2=0.0,
+                    op0=ALU.mult,
+                    op1=ALU.add,
                 )
 
-        def regroup_f1(s):
-            share = scalar_share(s)
+        def regroup_scalar(s):
+            first = G_COLS if beside_scores(s) else 0
+            nc.scalar.copy(
+                out=words_first(f_grouped[(s, 2)][:, first:, :]), in_=rows_first(f_raw[s][1][:, :, first:])
+            )
+            if beside_scores(s) and S_COLS:
+                nc.scalar.copy(
+                    out=words_first(f_grouped[(s, 1)][:, :S_COLS, :]), in_=rows_first(f_raw[s][0][:, :, :S_COLS])
+                )
+
+        def regroup_vector(s):
+            first = S_COLS if beside_scores(s) else 0
             nc.vector.tensor_copy(
-                out=words_first(f_grouped[(s, 1)][:, share:, :]), in_=rows_first(f_raw.pop(s)[0][:, :, share:])
+                out=words_first(f_grouped[(s, 1)][:, first:, :]), in_=rows_first(f_raw.pop(s)[0][:, :, first:])
             )
 
         def quantise_f(s, which):
@@ -219,23 +235,9 @@ def tile_multiheadattention_pa_kernel(tc, K, Q, F1, F2, out):
             a2[h] = soft.tile([P, PACK, TOKENS], BF16, name="a2")
 
         def normalise(h, j):
-            if j < PACK // 2:
-                nc.vector.tensor_scalar(
-                    out=a2[h][:, j, :],
-                    in0=expo[h][:, j, :],
-                    scalar1=inverse[h][:, j : j + 1],
-                    scalar2=None,
-                    op0=ALU.mult,
-                )
-            else:
-                nc.gpsimd.tensor_scalar(
-                    out=a2[h][:, j, :],
-                    in0=expo[h][:, j, :],
-                    scalar1=inverse[h][:, j : j + 1],
-                    scalar2=0.0,
-                    op0=ALU.mult,
-                    op1=ALU.add,
-                )
+            nc.scalar.activation(
+                out=a2[h][:, j, :], in_=expo[h][:, j, :], func=ACT.Copy, scale=inverse[h][:, j : j + 1]
+            )
 
         def flip_a2(h, pair):
             a2_words = a2[h][:].bitcast(F32).rearrange("m j (p u) -> m j u p", u=2)
@@ -279,11 +281,6 @@ def tile_multiheadattention_pa_kernel(tc, K, Q, F1, F2, out):
             if 0 <= s < STEPS:
                 action(s, *args)
 
-        def step_of(t):
-            if t + 1 < HEADS:
-                return t + 1
-            return t if t >= HEADS else -1
-
         load_qk(0, 1)
         load_f(0)
         load_qk(1, HEADS // 2)
@@ -292,31 +289,35 @@ def tile_multiheadattention_pa_kernel(tc, K, Q, F1, F2, out):
         for s in range(2, AHEAD - 1):
             load_f(s)
 
+        def product_of(t):
+            s = t - 3
+            return {HEADS - 1: HEADS, HEADS: HEADS - 1}.get(s, s)
+
         for t in range(-1, STEPS + 5):
             for_step(t + AHEAD, load_f)
-            for_head(t - 1, invert_sums)
-            for_head(t - 1, normalise, 2)
-            for_head(t - 1, normalise, 3)
+            for_step(t, quantise_f, 1)
+            for_step(t, quantise_f, 2)
+            for_step(t + 1, open_step)
+            for_step(t + 1, regroup_gpsimd)
+            for j in range(PACK):
+                for_head(t - 1, normalise, j)
+            for_step(product_of(t), multiply, 1)
             for j in range(PACK):
                 for_head(t, shifted, j)
                 for_head(t, exponential, j)
-            for_head(t - 1, normalise, 0)
-            for_head(t - 1, normalise, 1)
-            for_head(t + 1, flip_qk)
-            for_step(t - 3, multiply, 1)
-            for_head(t + 1, copy_qk)
-            for_head(t - 1, flip_a2, 2)
             for_head(t - 1, flip_a2, 0)
-            for_head(t - 1, copy_by_key, 2)
+            for_head(t - 1, flip_a2, 2)
+            for_head(t + 1, flip_qk)
+            for_step(product_of(t), multiply, 2)
+            for_head(t + 1, copy_qk)
             for_head(t - 1, copy_by_key, 0)
-            for_head(t - 2, quantise_by_query)
-            for_head(t - 2, quantise_by_key)
-            for_step(t - 3, multiply, 2)
+            for_head(t - 1, copy_by_key, 2)
             for j in range(PACK):
                 for_head(t + 1, score, j)
-            for_step(step_of(t - 1), quantise_f, 1)
-            for_step(step_of(t - 1), quantise_f, 2)
-            for_step(step_of(t), regroup_f2)
-            for_step(step_of(t), regroup_f1)
+            for_head(t - 2, quantise_by_query)
+            for_head(t - 2, quantise_by_key)
+            for_step(t + 1, regroup_scalar)
+            for_step(t + 1, regroup_vector)
+            for_head(t, invert_sums)
             for_head(t - 1, regroup_by_query)
-            for_step(t - 4, store_half)
+            for_step(product_of(t - 1), store_half)

@@ -22,8 +22,9 @@ BETA = 1.0 / (Z**0.5)
 RUN = 4
 STEPS = 2 * HEADS
 AHEAD = 8
-G_COLS = 384
-S_COLS = 64
+G_COLS = 320
+S_COLS = 0
+EARLY = 2
 
 FLOPS = 2 * HEADS * TOKENS * TOKENS * Z + 2 * 2 * HEADS * TOKENS * TOKENS * D
 
@@ -104,7 +105,7 @@ def tile_multiheadattention_pa_kernel(tc, K, Q, F1, F2, out):
             f_raw[s] = (f1_raw, f2_raw)
 
         def beside_scores(s):
-            return 1 <= s <= HEADS
+            return s < HEADS
 
         def open_step(s):
             pool = single_pool if beside_scores(s) else grouped_pool
@@ -122,20 +123,32 @@ def tile_multiheadattention_pa_kernel(tc, K, Q, F1, F2, out):
                     op1=ALU.add,
                 )
 
+        def shares(s):
+            if not beside_scores(s):
+                return 0, HALF, 0
+            if s < EARLY:
+                return G_COLS, G_COLS, 0
+            return G_COLS, HALF, S_COLS
+
         def regroup_scalar(s):
-            first = G_COLS if beside_scores(s) else 0
-            nc.scalar.copy(
-                out=words_first(f_grouped[(s, 2)][:, first:, :]), in_=rows_first(f_raw[s][1][:, :, first:])
-            )
-            if beside_scores(s) and S_COLS:
+            first, last, share = shares(s)
+            if first < last:
                 nc.scalar.copy(
-                    out=words_first(f_grouped[(s, 1)][:, :S_COLS, :]), in_=rows_first(f_raw[s][0][:, :, :S_COLS])
+                    out=words_first(f_grouped[(s, 2)][:, first:last, :]), in_=rows_first(f_raw[s][1][:, :, first:last])
+                )
+            if share:
+                nc.scalar.copy(
+                    out=words_first(f_grouped[(s, 1)][:, :share, :]), in_=rows_first(f_raw[s][0][:, :, :share])
                 )
 
         def regroup_vector(s):
-            first = S_COLS if beside_scores(s) else 0
+            first, last, share = shares(s)
+            if last < HALF:
+                nc.vector.tensor_copy(
+                    out=words_first(f_grouped[(s, 2)][:, last:, :]), in_=rows_first(f_raw[s][1][:, :, last:])
+                )
             nc.vector.tensor_copy(
-                out=words_first(f_grouped[(s, 1)][:, first:, :]), in_=rows_first(f_raw.pop(s)[0][:, :, first:])
+                out=words_first(f_grouped[(s, 1)][:, share:, :]), in_=rows_first(f_raw.pop(s)[0][:, :, share:])
             )
 
         def quantise_f(s, which):
@@ -283,10 +296,12 @@ def tile_multiheadattention_pa_kernel(tc, K, Q, F1, F2, out):
 
         load_qk(0, 1)
         load_f(0)
-        load_qk(1, HEADS // 2)
+        load_qk(1, 2)
         load_f(1)
+        load_qk(2, HEADS // 2)
+        load_f(2)
         load_qk(HEADS // 2, HEADS)
-        for s in range(2, AHEAD - 1):
+        for s in range(3, AHEAD - 1):
             load_f(s)
 
         def product_of(t):
@@ -295,10 +310,10 @@ def tile_multiheadattention_pa_kernel(tc, K, Q, F1, F2, out):
 
         for t in range(-1, STEPS + 5):
             for_step(t + AHEAD, load_f)
-            for_step(t, quantise_f, 1)
-            for_step(t, quantise_f, 2)
-            for_step(t + 1, open_step)
-            for_step(t + 1, regroup_gpsimd)
+            for_step(t - 1, quantise_f, 1)
+            for_step(t - 1, quantise_f, 2)
+            for_step(t, open_step)
+            for_step(t, regroup_gpsimd)
             for j in range(PACK):
                 for_head(t - 1, normalise, j)
             for_step(product_of(t), multiply, 1)
@@ -316,8 +331,8 @@ def tile_multiheadattention_pa_kernel(tc, K, Q, F1, F2, out):
                 for_head(t + 1, score, j)
             for_head(t - 2, quantise_by_query)
             for_head(t - 2, quantise_by_key)
-            for_step(t + 1, regroup_scalar)
-            for_step(t + 1, regroup_vector)
+            for_step(t, regroup_scalar)
+            for_step(t, regroup_vector)
             for_head(t, invert_sums)
             for_head(t - 1, regroup_by_query)
             for_step(product_of(t - 1), store_half)

@@ -24,6 +24,7 @@ STEPS = 2 * HEADS
 AHEAD = 8
 G_COLS = 320
 S_COLS = 0
+LATE_COLS = 32
 EARLY = 2
 
 FLOPS = 2 * HEADS * TOKENS * TOKENS * Z + 2 * 2 * HEADS * TOKENS * TOKENS * D
@@ -99,9 +100,13 @@ def tile_multiheadattention_pa_kernel(tc, K, Q, F1, F2, out):
             h = s % HEADS
             cols = slice((s // HEADS) * HALF, (s // HEADS + 1) * HALF)
             f2_raw = raw_pool.tile([P, PACK, HALF], BF16)
-            nc.sync.dma_start(out=f2_raw[:], in_=f2_rows[:, :, h, cols])
             f1_raw = raw_pool.tile([P, PACK, HALF], BF16)
-            nc.sync.dma_start(out=f1_raw[:], in_=f1_rows[:, :, h, cols])
+            if s == 0:
+                nc.sync.dma_start(out=f1_raw[:], in_=f1_rows[:, :, h, cols])
+                nc.sync.dma_start(out=f2_raw[:], in_=f2_rows[:, :, h, cols])
+            else:
+                nc.sync.dma_start(out=f2_raw[:], in_=f2_rows[:, :, h, cols])
+                nc.sync.dma_start(out=f1_raw[:], in_=f1_rows[:, :, h, cols])
             f_raw[s] = (f1_raw, f2_raw)
 
         def beside_scores(s):
@@ -125,31 +130,34 @@ def tile_multiheadattention_pa_kernel(tc, K, Q, F1, F2, out):
 
         def shares(s):
             if not beside_scores(s):
-                return 0, HALF, 0
+                return 0, HALF, LATE_COLS
             if s < EARLY:
                 return G_COLS, G_COLS, 0
             return G_COLS, HALF, S_COLS
 
         def regroup_scalar(s):
             first, last, share = shares(s)
-            if first < last:
-                nc.scalar.copy(
-                    out=words_first(f_grouped[(s, 2)][:, first:last, :]), in_=rows_first(f_raw[s][1][:, :, first:last])
-                )
             if share:
                 nc.scalar.copy(
                     out=words_first(f_grouped[(s, 1)][:, :share, :]), in_=rows_first(f_raw[s][0][:, :, :share])
                 )
+            if first < last:
+                nc.scalar.copy(
+                    out=words_first(f_grouped[(s, 2)][:, first:last, :]), in_=rows_first(f_raw[s][1][:, :, first:last])
+                )
 
-        def regroup_vector(s):
+        def regroup_vector_f1(s):
+            first, last, share = shares(s)
+            nc.vector.tensor_copy(
+                out=words_first(f_grouped[(s, 1)][:, share:, :]), in_=rows_first(f_raw[s][0][:, :, share:])
+            )
+
+        def regroup_vector_f2(s):
             first, last, share = shares(s)
             if last < HALF:
                 nc.vector.tensor_copy(
                     out=words_first(f_grouped[(s, 2)][:, last:, :]), in_=rows_first(f_raw[s][1][:, :, last:])
                 )
-            nc.vector.tensor_copy(
-                out=words_first(f_grouped[(s, 1)][:, share:, :]), in_=rows_first(f_raw.pop(s)[0][:, :, share:])
-            )
 
         def quantise_f(s, which):
             codes = codes_pool.tile([P, HALF], U32, align_bytes=64, name="f%d_codes" % which)
@@ -304,26 +312,29 @@ def tile_multiheadattention_pa_kernel(tc, K, Q, F1, F2, out):
         for s in range(3, AHEAD - 1):
             load_f(s)
 
-        def product_of(t):
-            s = t - 3
-            return {HEADS - 1: HEADS, HEADS: HEADS - 1}.get(s, s)
+        def products_of(t):
+            if t - 2 < HEADS - 1:
+                return [t - 2]
+            if t - 2 == HEADS - 1:
+                return [HEADS, HEADS - 1]
+            return [t - 1]
 
         for t in range(-1, STEPS + 5):
             for_step(t + AHEAD, load_f)
             for_step(t - 1, quantise_f, 1)
             for_step(t - 1, quantise_f, 2)
             for_step(t, open_step)
+            if t == 0:
+                regroup_vector_f1(t)
             for_step(t, regroup_gpsimd)
             for j in range(PACK):
                 for_head(t - 1, normalise, j)
-            for_step(product_of(t), multiply, 1)
             for j in range(PACK):
                 for_head(t, shifted, j)
                 for_head(t, exponential, j)
             for_head(t - 1, flip_a2, 0)
             for_head(t - 1, flip_a2, 2)
             for_head(t + 1, flip_qk)
-            for_step(product_of(t), multiply, 2)
             for_head(t + 1, copy_qk)
             for_head(t - 1, copy_by_key, 0)
             for_head(t - 1, copy_by_key, 2)
@@ -331,8 +342,14 @@ def tile_multiheadattention_pa_kernel(tc, K, Q, F1, F2, out):
                 for_head(t + 1, score, j)
             for_head(t - 2, quantise_by_query)
             for_head(t - 2, quantise_by_key)
+            for s in products_of(t):
+                for_step(s, multiply, 1)
+                for_step(s, multiply, 2)
             for_step(t, regroup_scalar)
-            for_step(t, regroup_vector)
+            for_step(t, regroup_vector_f2)
+            if t != 0:
+                for_step(t, regroup_vector_f1)
             for_head(t, invert_sums)
             for_head(t - 1, regroup_by_query)
-            for_step(product_of(t - 1), store_half)
+            for s in products_of(t - 1):
+                for_step(s, store_half)

@@ -329,6 +329,7 @@ def tile_multiheadattention_pa_kernel(tc, K, Q, F1, F2, out):
             for_step(t, regroup_gpsimd)
             for j in range(PACK):
                 for_head(t - 1, normalise, j)
+            for_step(t, regroup_scalar)
             for j in range(PACK):
                 for_head(t, shifted, j)
                 for_head(t, exponential, j)
@@ -345,7 +346,6 @@ def tile_multiheadattention_pa_kernel(tc, K, Q, F1, F2, out):
             for s in products_of(t):
                 for_step(s, multiply, 1)
                 for_step(s, multiply, 2)
-            for_step(t, regroup_scalar)
             for_step(t, regroup_vector_f2)
             if t != 0:
                 for_step(t, regroup_vector_f1)

@@ -194,32 +194,40 @@ def tile_multiheadattention_pa_kernel(tc, K, Q, F1, F2, out):
                 return
             acc = banks_of(s)
             cols = slice((s // HEADS) * HALF, (s // HEADS + 1) * HALF)
+            at_end = s == STEPS - 1
             for i in range(PACK):
                 result = results.tile([P, HALF], F32)
-                if i % 2 == 0:
+                if (i % 2 == 1) == at_end:
                     nc.scalar.mul(out=result[:], in_=acc[i][:], mul=-1.0)
+                    queue = nc.scalar if at_end else nc.sync
                 else:
                     nc.vector.tensor_scalar_mul(out=result[:], in0=acc[i][:], scalar1=-1.0)
-                nc.sync.dma_start(out=out_rows[:, i, cols], in_=result[:])
+                    queue = nc.sync
+                queue.dma_start(out=out_rows[:, i, cols], in_=result[:])
 
         def flip_qk(h):
-            flipped = work.tile([P, 2, PACK, P], BF16, tag="work")
+            flipped = work.tile([P, 2 * PACK, P], BF16, tag="work")
             for j in range(PACK):
-                nc.tensor.transpose(flipped[:, 0, j, :], q_raw[:, j, h, :], ident[:])
-                nc.tensor.transpose(flipped[:, 1, j, :], k_raw[:, j, h, :], ident[:])
+                nc.tensor.transpose(flipped[:, j, :], k_raw[:, j, h, :], ident[:])
+            for j in range(PACK):
+                nc.tensor.transpose(flipped[:, PACK + j, :], q_raw[:, j, h, :], ident[:])
             flipped_qk[h] = flipped
 
         def copy_qk(h):
-            qk = soft.tile([P, 2, PACK, P], BF16)
-            nc.scalar.copy(out=qk[:], in_=flipped_qk.pop(h)[:])
+            qk = soft.tile([P, 2 * PACK, P], BF16)
+            flipped = flipped_qk.pop(h)
+            cut = PACK + 1 if h == 0 else 2 * PACK
+            nc.scalar.copy(out=qk[:, :cut, :], in_=flipped[:, :cut, :])
+            if cut < 2 * PACK:
+                nc.scalar.copy(out=qk[:, cut:, :], in_=flipped[:, cut:, :])
             qk_t[h] = qk
 
         def score(h, j):
             bank = work.tile([P, TOKENS], F32, tag="work")
             nc.tensor.matmul(
                 out=bank[:],
-                lhsT=qk_t[h][:, 0, j, :],
-                rhs=qk_t[h][:, 1, :, :].rearrange("z j p -> z (j p)"),
+                lhsT=qk_t[h][:, PACK + j, :],
+                rhs=qk_t[h][:, :PACK, :].rearrange("z j p -> z (j p)"),
                 start=True,
                 stop=True,
             )

from contextlib import ExitStack

import concourse.mybir as mybir
from concourse.masks import make_identity

BF16 = mybir.dt.bfloat16
F32 = mybir.dt.float32
U32 = mybir.dt.uint32
U8 = mybir.dt.uint8
FP8X4 = mybir.dt.float8_e4m3fn_x4
ALU = mybir.AluOpType
ACT = mybir.ActivationFunctionType

P = 128
PACK = 4
TOKENS = P * PACK
HEADS = 8
Z = 128
D = 1024
HALF = 512
BETA = 1.0 / (Z**0.5)
RUN = 4
STEPS = 2 * HEADS
AHEAD = 8
G_COLS = 320
S_COLS = 0
LATE_COLS = 32
EARLY = 2

FLOPS = 2 * HEADS * TOKENS * TOKENS * Z + 2 * 2 * HEADS * TOKENS * TOKENS * D


def words_first(grouped):
    return grouped.rearrange("p (c i) t -> p c t i", i=RUN)


def rows_first(raw):
    return raw.rearrange("p t (c i) -> p c t i", i=RUN)


def tile_multiheadattention_pa_kernel(tc, K, Q, F1, F2, out):
    nc = tc.nc

    q_rows = Q.rearrange("(j p) h z -> p j h z", p=P)
    k_rows = K.rearrange("(j p) h z -> p j h z", p=P)
    f1_rows = F1.rearrange("(p j) h d -> p j h d", j=PACK)
    f2_rows = F2.rearrange("(j p) h d -> p j h d", p=P)
    out_rows = out.rearrange("(j p) d -> p j d", p=P)

    with ExitStack() as ctx:
        ctx.enter_context(tc.manual_schedule())
        keep = ctx.enter_context(tc.tile_pool(name="keep", bufs=1))
        raw_pool = ctx.enter_context(tc.tile_pool(name="raw", bufs=AHEAD + 1))
        soft = ctx.enter_context(tc.tile_pool(name="soft", bufs=2))
        grouped_pool = ctx.enter_context(tc.tile_pool(name="grouped", bufs=2))
        single_pool = ctx.enter_context(tc.tile_pool(name="single", bufs=1))
        codes_pool = ctx.enter_context(tc.tile_pool(name="codes", bufs=5))
        results = ctx.enter_context(tc.tile_pool(name="results", bufs=PACK))
        acc_pool = ctx.enter_context(tc.psum_pool(name="acc", bufs=1))
        work = ctx.enter_context(tc.psum_pool(name="work", bufs=PACK))

        q_raw = keep.tile([P, PACK, HEADS, Z], BF16)
        k_raw = keep.tile([P, PACK, HEADS, Z], BF16)
        ident = keep.tile([P, P], BF16)
        make_identity(nc, ident[:])
        ident_words = keep.tile([P, P], F32)
        make_identity(nc, ident_words[:])

        by_key_codes = keep.tile([P, HEADS, TOKENS], U32, align_bytes=64)
        by_key_scales = keep.tile([P, HEADS, TOKENS], U8, align_bytes=64)
        by_query_codes = keep.tile([P, HEADS, TOKENS], U32, align_bytes=64)
        by_query_scales = keep.tile([P, HEADS, TOKENS], U8, align_bytes=64)

        acc_lo = [acc_pool.tile([P, HALF], F32, name="acc_lo%d" % i) for i in range(PACK)]
        acc_hi = []

        f_raw = {}
        f_grouped = {}
        f_quantised = {}
        flipped_qk = {}
        qk_t = {}
        scores = {}
        expo = {}
        shift = {}
        sums = {}
        inverse = {}
        a2 = {}
        flipped_a2 = {}
        by_key = {}
        by_query = {}

        def quantise(grouped, codes, scales):
            nc.vector.quantize_mx(out=codes.bitcast(FP8X4), scales=scales, in_=grouped)

        def load_qk(first, last):
            nc.sync.dma_start(out=k_raw[:, :, first:last, :], in_=k_rows[:, :, first:last, :])
            nc.sync.dma_start(out=q_raw[:, :, first:last, :], in_=q_rows[:, :, first:last, :])

        def load_f(s):
            h = s % HEADS
            cols = slice((s // HEADS) * HALF, (s // HEADS + 1) * HALF)
            f2_raw = raw_pool.tile([P, PACK, HALF], BF16)
            f1_raw = raw_pool.tile([P, PACK, HALF], BF16)
            if s == 0:
                nc.sync.dma_start(out=f1_raw[:], in_=f1_rows[:, :, h, cols])
                nc.sync.dma_start(out=f2_raw[:], in_=f2_rows[:, :, h, cols])
            else:
                nc.sync.dma_start(out=f2_raw[:], in_=f2_rows[:, :, h, cols])
                nc.sync.dma_start(out=f1_raw[:], in_=f1_rows[:, :, h, cols])
            f_raw[s] = (f1_raw, f2_raw)

        def beside_scores(s):
            return s < HEADS

        def open_step(s):
            pool = single_pool if beside_scores(s) else grouped_pool
            f_grouped[(s, 2)] = pool.tile([P, HALF, PACK], BF16, align_bytes=64, name="f2_grouped")
            f_grouped[(s, 1)] = grouped_pool.tile([P, HALF, PACK], BF16, align_bytes=64, name="f1_grouped")

        def regroup_gpsimd(s):
            if beside_scores(s):
                nc.gpsimd.tensor_scalar(
                    out=f_grouped[(s, 2)][:, :G_COLS, :],
                    in0=f_raw[s][1][:, :, :G_COLS].rearrange("p t c -> p c t"),
                    scalar1=1.0,
                    scalar2=0.0,
                    op0=ALU.mult,
                    op1=ALU.add,
                )

        def shares(s):
            if not beside_scores(s):
                return 0, HALF, LATE_COLS
            if s < EARLY:
                return G_COLS, G_COLS, 0
            return G_COLS, HALF, S_COLS

        def regroup_scalar(s):
            first, last, share = shares(s)
            if share:
                nc.scalar.copy(
                    out=words_first(f_grouped[(s, 1)][:, :share, :]), in_=rows_first(f_raw[s][0][:, :, :share])
                )
            if first < last:
                nc.scalar.copy(
                    out=words_first(f_grouped[(s, 2)][:, first:last, :]), in_=rows_first(f_raw[s][1][:, :, first:last])
                )

        def regroup_vector_f1(s):
            first, last, share = shares(s)
            nc.vector.tensor_copy(
                out=words_first(f_grouped[(s, 1)][:, share:, :]), in_=rows_first(f_raw[s][0][:, :, share:])
            )

        def regroup_vector_f2(s):
            first, last, share = shares(s)
            if last < HALF:
                nc.vector.tensor_copy(
                    out=words_first(f_grouped[(s, 2)][:, last:, :]), in_=rows_first(f_raw[s][1][:, :, last:])
                )

        def quantise_f(s, which):
            codes = codes_pool.tile([P, HALF], U32, align_bytes=64, name="f%d_codes" % which)
            scales = codes_pool.tile([P, HALF], U8, align_bytes=64, name="f%d_scales" % which)
            quantise(f_grouped.pop((s, which))[:].rearrange("p c t -> p (c t)"), codes[:], scales[:])
            f_quantised[(s, which)] = (codes, scales)

        def banks_of(s):
            if s < HEADS:
                return acc_lo
            if not acc_hi:
                acc_hi.extend(work.tile([P, HALF], F32, tag="work", name="acc_hi%d" % i) for i in range(PACK))
            return acc_hi

        def multiply(s, which):
            h = s % HEADS
            acc = banks_of(s)
            a2_codes, a2_scales = (by_key_codes, by_key_scales) if which == 1 else (by_query_codes, by_query_scales)
            f_codes, f_scales = f_quantised.pop((s, which))
            for i in range(PACK):
                rows = slice(i * P, (i + 1) * P)
                nc.tensor.matmul_mx(
                    out=acc[i][:],
                    lhsT=a2_codes[:, h, rows].bitcast(FP8X4),
                    lhsT_scale=a2_scales[:, h, rows],
                    rhs=f_codes[:].bitcast(FP8X4),
                    rhs_scale=f_scales[:],
                    start=(h == 0 and which == 1),
                    stop=(h == HEADS - 1 and which == 2),
                )

        def store_half(s):
            if s % HEADS != HEADS - 1:
                return
            acc = banks_of(s)
            cols = slice((s // HEADS) * HALF, (s // HEADS + 1) * HALF)
            at_end = s == STEPS - 1
            for i in range(PACK):
                result = results.tile([P, HALF], F32)
                if (i % 2 == 1) == at_end:
                    nc.scalar.mul(out=result[:], in_=acc[i][:], mul=-1.0)
                    queue = nc.scalar if at_end else nc.sync
                else:
                    nc.vector.tensor_scalar_mul(out=result[:], in0=acc[i][:], scalar1=-1.0)
                    queue = nc.sync
                queue.dma_start(out=out_rows[:, i, cols], in_=result[:])

        def flip_qk(h):
            flipped = work.tile([P, 2 * PACK, P], BF16, tag="work")
            for j in range(PACK):
                nc.tensor.transpose(flipped[:, j, :], k_raw[:, j, h, :], ident[:])
            for j in range(PACK):
                nc.tensor.transpose(flipped[:, PACK + j, :], q_raw[:, j, h, :], ident[:])
            flipped_qk[h] = flipped

        def copy_qk(h):
            qk = soft.tile([P, 2 * PACK, P], BF16)
            flipped = flipped_qk.pop(h)
            cut = PACK + 1 if h == 0 else 2 * PACK
            nc.scalar.copy(out=qk[:, :cut, :], in_=flipped[:, :cut, :])
            if cut < 2 * PACK:
                nc.scalar.copy(out=qk[:, cut:, :], in_=flipped[:, cut:, :])
            qk_t[h] = qk

        def score(h, j):
            bank = work.tile([P, TOKENS], F32, tag="work")
            nc.tensor.matmul(
                out=bank[:],
                lhsT=qk_t[h][:, PACK + j, :],
                rhs=qk_t[h][:, :PACK, :].rearrange("z j p -> z (j p)"),
                start=True,
                stop=True,
            )
            scores[(h, j)] = bank

        def shifted(h, j):
            if j == 0:
                expo[h] = soft.tile([P, PACK, TOKENS], F32, name="expo")
                shift[h] = soft.tile([P, PACK], F32, name="shift")
                sums[h] = soft.tile([P, PACK], F32, name="sums")
            nc.vector.tensor_scalar(
                out=expo[h][:, j, :],
                in0=scores.pop((h, j))[:],
                scalar1=-BETA,
                scalar2=None,
                op0=ALU.mult,
                op1=ALU.min,
                accum_out=shift[h][:, j : j + 1],
            )

        def exponential(h, j):
            nc.scalar.activation(
                out=expo[h][:, j, :],
                in_=expo[h][:, j, :],
                func=ACT.Exp,
                bias=shift[h][:, j : j + 1],
                scale=-1.0,
                accum_out=sums[h][:, j : j + 1],
            )

        def invert_sums(h):
            inverse[h] = soft.tile([P, PACK], F32, name="inverse")
            nc.vector.reciprocal(out=inverse[h][:], in_=sums[h][:])
            a2[h] = soft.tile([P, PACK, TOKENS], BF16, name="a2")

        def normalise(h, j):
            nc.scalar.activation(
                out=a2[h][:, j, :], in_=expo[h][:, j, :], func=ACT.Copy, scale=inverse[h][:, j : j + 1]
            )

        def flip_a2(h, pair):
            a2_words = a2[h][:].bitcast(F32).rearrange("m j (p u) -> m j u p", u=2)
            flipped = work.tile([P, 2, 2, P], F32, tag="work")
            for a in range(2):
                for u in range(2):
                    nc.tensor.transpose(flipped[:, a, u, :], a2_words[:, pair + a, u, :], ident_words[:])
            flipped_a2[(h, pair)] = flipped

        def copy_by_key(h, pair):
            if h not in by_key:
                by_key[h] = soft.tile([P, PACK, P, PACK], BF16, align_bytes=64, name="by_key")
            nc.scalar.copy(
                out=by_key[h][:, pair : pair + 2, :, :].bitcast(F32),
                in_=flipped_a2.pop((h, pair))[:].rearrange("p a u m -> p a m u"),
            )

        def regroup_by_query(h):
            by_query[h] = soft.tile([P, TOKENS, PACK], BF16, align_bytes=64, name="by_query")
            nc.vector.tensor_copy(out=words_first(by_query[h][:]), in_=rows_first(a2[h][:]))

        def quantise_by_query(h):
            quantise(
                by_query.pop(h)[:].rearrange("p c t -> p (c t)"),
                by_query_codes[:, h, :],
                by_query_scales[:, h, :],
            )

        def quantise_by_key(h):
            quantise(
                by_key.pop(h)[:].rearrange("p j m t -> p (j m t)"),
                by_key_codes[:, h, :],
                by_key_scales[:, h, :],
            )

        def for_head(h, action, *args):
            if 0 <= h < HEADS:
                action(h, *args)

        def for_step(s, action, *args):
            if 0 <= s < STEPS:
                action(s, *args)

        load_qk(0, 1)
        load_f(0)
        load_qk(1, 2)
        load_f(1)
        load_qk(2, HEADS // 2)
        load_f(2)
        load_qk(HEADS // 2, HEADS)
        for s in range(3, AHEAD - 1):
            load_f(s)

        def products_of(t):
            if t - 2 < HEADS - 1:
                return [t - 2]
            if t - 2 == HEADS - 1:
                return [HEADS, HEADS - 1]
            return [t - 1]

        for t in range(-1, STEPS + 5):
            for_step(t + AHEAD, load_f)
            for_step(t - 1, quantise_f, 1)
            for_step(t - 1, quantise_f, 2)
            for_step(t, open_step)
            if t == 0:
                regroup_vector_f1(t)
            for_step(t, regroup_gpsimd)
            for j in range(PACK):
                for_head(t - 1, normalise, j)
            for_step(t, regroup_scalar)
            for j in range(PACK):
                for_head(t, shifted, j)
                for_head(t, exponential, j)
            for_head(t - 1, flip_a2, 0)
            for_head(t - 1, flip_a2, 2)
            for_head(t + 1, flip_qk)
            for_head(t + 1, copy_qk)
            for_head(t - 1, copy_by_key, 0)
            for_head(t - 1, copy_by_key, 2)
            for j in range(PACK):
                for_head(t + 1, score, j)
            for_head(t - 2, quantise_by_query)
            for_head(t - 2, quantise_by_key)
            for s in products_of(t):
                for_step(s, multiply, 1)
                for_step(s, multiply, 2)
            for_step(t, regroup_vector_f2)
            if t != 0:
                for_step(t, regroup_vector_f1)
            for_head(t, invert_sums)
            for_head(t - 1, regroup_by_query)
            for s in products_of(t - 1):
                for_step(s, store_half)
